import numpy as np
import ml_dtypes


def mxq(x, axis, fmt="e4m3"):
    dtype, down = {"e4m3": (ml_dtypes.float8_e4m3fn, 7), "e5m2": (ml_dtypes.float8_e5m2, 14)}[fmt]
    v = np.moveaxis(np.asarray(x, np.float32).astype(ml_dtypes.bfloat16).astype(np.float64), axis, -1)
    blocks = v.reshape(v.shape[:-1] + (-1, 32))
    amax = np.abs(blocks).max(-1, keepdims=True)
    byte = np.maximum(np.where(amax > 0, np.frexp(amax)[1] - 1 + 127, 0) - down, 1)
    scale = np.exp2(byte - 127.0)
    codes = (blocks / scale).astype(np.float32).astype(dtype).astype(np.float64)
    return np.moveaxis((codes * scale).reshape(v.shape), -1, axis)


WIDE = False


def mx_kscale(k):
    if not WIDE:
        return np.ones(k)
    levels = np.array([10, -10, 5, -5, 0])
    a = np.random.permutation(np.resize(levels, k // 512 * 4)).reshape(k // 512, 4)
    idx = np.arange(k)
    return np.exp2(a[idx // 512, idx % 128 // 32])


BF16 = ml_dtypes.bfloat16


def bf(x):
    return np.asarray(x, np.float32).astype(BF16)


def f64(x):
    return np.asarray(x).astype(np.float64)


E2M1 = np.array([0.0, 0.5, 1.0, 1.5, 2.0, 3.0, 4.0, 6.0, -0.0, -0.5, -1.0, -1.5, -2.0, -3.0, -4.0, -6.0])


def pack_weight(w, fmt):
    k, n = w.shape
    w = f64(bf(w)).reshape(k // 32, 32, n)
    amax = np.abs(w).max(1)
    if fmt == "e4m3":
        byte = np.frexp(amax)[1] - 1 + 127 - 7
    else:
        mant, ex = np.frexp(amax / 6.0)
        byte = np.where(mant > 0.5, ex, ex - 1) + 127
    byte = np.clip(np.where(amax > 0, byte, 1), 1, 254)
    scaled = (w * np.exp2(127.0 - byte)[:, None, :]).reshape(k, n).astype(np.float32)
    by_word = np.ascontiguousarray(scaled.reshape(k // 512, 128, 4, n).transpose(0, 1, 3, 2))
    if fmt == "e4m3":
        words = by_word.astype(ml_dtypes.float8_e4m3fn).view(np.uint8)
    else:
        c = by_word.astype(ml_dtypes.float4_e2m1fn).view(np.uint8) & 0xF
        words = c[..., 0::2] | (c[..., 1::2] << 4)
    return np.ascontiguousarray(words), np.ascontiguousarray(byte.astype(np.uint8).reshape(k // 512, 16, n))


def unpack_weight(words, scales, fmt):
    g, p, n, _ = words.shape
    if fmt == "e4m3":
        vals = np.ascontiguousarray(words).view(ml_dtypes.float8_e4m3fn).astype(np.float64)
    else:
        nib = np.empty((g, p, n, 4), np.uint8)
        nib[..., 0::2] = words & 0xF
        nib[..., 1::2] = words >> 4
        vals = E2M1[nib]
    vals = vals * np.repeat(np.exp2(scales.astype(np.float64) - 127.0), 8, axis=1)[..., None]
    return vals.transpose(0, 1, 3, 2).reshape(g * 512, n)


NUM_PLANES = 80
BOARD = 8 * 8
IN_DIM = NUM_PLANES * BOARD
OUT_DIM = 1920
B = 512
FMT = "e4m3"


def setup_inputs():
    s = mx_kscale(IN_DIM)
    x = np.random.standard_normal((B, NUM_PLANES, 8, 8)) * s.reshape(NUM_PLANES, 8, 8)
    rows = np.random.randint(0, IN_DIM, size=OUT_DIM)
    m = np.random.standard_normal((IN_DIM, OUT_DIM)) * 0.01
    m[rows, np.arange(OUT_DIM)] += 1.0
    words, scales = pack_weight(m / s[:, None], FMT)
    return {"x": bf(x), "fc1_words": words, "fc1_scales": scales}


def reference(x, fc1_words, fc1_scales):
    h = f64(x).reshape(-1, IN_DIM)
    return mxq(h, 1, "e4m3") @ unpack_weight(fc1_words, fc1_scales, FMT)

@@ -1,0 +1,193 @@
+from contextlib import ExitStack
+
+import concourse.mybir as mybir
+from concourse.masks import make_identity
+
+FP8X4 = mybir.dt.float8_e4m3fn_x4
+BF16 = mybir.dt.bfloat16
+F32 = mybir.dt.float32
+I32 = mybir.dt.int32
+U32 = mybir.dt.uint32
+U8 = mybir.dt.uint8
+
+P = 128
+ROWS = 512
+K = 5120
+N_OUT = 1920
+PASSES = 10
+M_TILES = 4
+FLOPS = 2 * ROWS * K * N_OUT
+
+N_CHUNKS = 5
+SORTED_FROM = 1
+
+
+def tile_applypolicymap_kernel(tc, x, fc1_words, fc1_scales, out):
+    nc = tc.nc
+    xf = x.rearrange("(m p) c h w -> p m (c h w)", p=P)
+    ww = fc1_words.rearrange("g p n t -> g p (n t)").bitcast(I32).rearrange("g p n -> p g n")
+
+    with ExitStack() as ctx:
+        const = ctx.enter_context(tc.tile_pool(name="const", bufs=1))
+        xs_pool = ctx.enter_context(tc.tile_pool(name="xs", bufs=4))
+        xg_pool = ctx.enter_context(tc.tile_pool(name="xg", bufs=4))
+        psum = ctx.enter_context(tc.psum_pool(name="psum", bufs=1))
+        ctx.enter_context(tc.manual_schedule())
+
+        warm_in = const.tile([P, 1], F32, name="warm_in")
+        warm_out = const.tile([P, 1], F32, name="warm_out")
+        nc.vector.memset(warm_in[:], 0.0)
+        nc.scalar.copy(out=warm_out[:], in_=warm_in[:])
+        pa = [const.tile([P, 512], U8, name="pa%d" % s, align_bytes=64) for s in range(3)]
+        pr = [const.tile([P, 1408], U8, name="pr%d" % s, align_bytes=64) for s in range(3)]
+        for t in pa + pr:
+            nc.vector.memset(t[:].bitcast(I32), 0)
+        ident = const.tile([P, P], F32, name="ident")
+        make_identity(nc, ident[:])
+
+        xr = {}
+        wa = []
+        wbc = []
+        wde = []
+
+        def load_x(c):
+            for j in range(2):
+                t = const.tile([P, 2, 1024], BF16, name="xr%d_%d" % (c, j))
+                nc.sync.dma_start(out=t[:], in_=xf[:, 2 * j : 2 * j + 2, 1024 * c : 1024 * (c + 1)])
+                xr[(c, j)] = t
+
+        def load_planes(tiles, s, c0, c1):
+            n_planes = min(4, PASSES - 4 * s)
+            for q in range(4):
+                nc.sync.dma_start(
+                    out=tiles[s][32 * q : 32 * q + 4 * n_planes, :].bitcast(I32),
+                    in_=fc1_scales[4 * s : 4 * s + n_planes, 4 * q : 4 * q + 4, c0:c1].bitcast(I32),
+                )
+
+        def load_wa(c):
+            t = const.tile([P, 2, 512], U32, name="wa%d" % c, align_bytes=64)
+            nc.sync.dma_start(out=t[:].bitcast(I32), in_=ww[:, 2 * c : 2 * c + 2, 0:512])
+            wa.append(t)
+
+        def load_wbc(g):
+            t = const.tile([P, 1024], U32, name="wbc%d" % g, align_bytes=64)
+            nc.sync.dma_start(out=t[:].bitcast(I32), in_=ww[:, g, 512:1536])
+            wbc.append(t)
+
+        def load_wde(h):
+            t = const.tile([P, 5, 384], U32, name="wde%d" % h, align_bytes=64)
+            nc.sync.dma_start(out=t[:].bitcast(I32), in_=ww[:, 5 * h : 5 * h + 5, 1536:1920])
+            wde.append(t)
+
+        load_x(0)
+        load_x(1)
+        load_planes(pa, 0, 0, 512)
+        load_wa(0)
+        load_x(2)
+        load_planes(pa, 1, 0, 512)
+        load_wa(1)
+        load_x(3)
+        load_wa(2)
+        load_x(4)
+        load_planes(pa, 2, 0, 512)
+        load_wa(3)
+        load_wa(4)
+        load_planes(pr, 0, 512, 1920)
+        for g in range(0, 4):
+            load_wbc(g)
+        load_planes(pr, 1, 512, 1920)
+        load_planes(pr, 2, 512, 1920)
+        for g in range(4, PASSES):
+            load_wbc(g)
+        load_wde(0)
+        load_wde(1)
+
+        xg = {}
+        xq = {}
+        xp = {}
+
+        def transposes(c):
+            for gi in range(2):
+                g = 2 * c + gi
+                xg[g] = xg_pool.tile([P, 2048], BF16, tag="xg", name="xg%d" % g, align_bytes=64)
+            for j in range(2):
+                xw = xr[(c, j)][:].rearrange("p m k -> p (m k)").bitcast(F32)
+                if c >= SORTED_FROM:
+                    xs = xs_pool.tile([P, 4, 2, P], F32, tag="xs", name="xs%d_%d" % (c, j))
+                    nc.vector.tensor_copy(out=xs[:], in_=xw.rearrange("p (a q u) -> p a u q", a=4, q=P, u=2))
+                for gi in range(2):
+                    g = 2 * c + gi
+                    bank = 2 * j + gi if c == 0 else 4 + 2 * j + gi
+                    tb = psum.tile([P, 2, 2, P], F32, tag="bank%d" % bank, name="tb%d_%d" % (g, j))
+                    for mi in range(2):
+                        a = 2 * mi + gi
+                        for u in range(2):
+                            if c >= SORTED_FROM:
+                                src = xs[:, a, u, :]
+                            else:
+                                src = xw[:, 256 * a + u : 256 * (a + 1) : 2]
+                            nc.tensor.transpose(tb[:, mi, u, :], src, ident[:])
+                    dst = xg[g][:].bitcast(F32).rearrange("p (m r u) -> p m r u", m=4, r=P, u=2)
+                    nc.scalar.copy(out=dst[:, 2 * j : 2 * j + 2], in_=tb[:].rearrange("p m u r -> p m r u"))
+
+        def quantise(c):
+            for gi in range(2):
+                g = 2 * c + gi
+                xq[g] = const.tile([P, ROWS], U32, name="xq%d" % g, align_bytes=64)
+                xp[g] = const.tile([P, ROWS], U8, name="xp%d" % g, align_bytes=64)
+                nc.vector.quantize_mx(out=xq[g][:].bitcast(FP8X4), scales=xp[g][:], in_=xg[g][:])
+
+        def mx(acc, g, m, rhs, planes, col0, width):
+            k = 4 * (g % 4)
+            nc.tensor.matmul_mx(
+                out=acc,
+                lhsT=xq[g][:, P * m : P * (m + 1)].bitcast(FP8X4),
+                lhsT_scale=xp[g][:, P * m : P * (m + 1)],
+                rhs=rhs.bitcast(FP8X4),
+                rhs_scale=planes[g // 4][k:P, col0 : col0 + width],
+                start=(g == 0),
+                stop=(g == PASSES - 1),
+            )
+
+        def evacuate(acc, m, n0, width, on_scalar):
+            ob = const.tile([P, width], F32, name="ob%d_%d" % (m, n0))
+            if on_scalar:
+                nc.scalar.copy(out=ob[:], in_=acc)
+            else:
+                nc.vector.tensor_copy(out=ob[:], in_=acc)
+            nc.sync.dma_start(out=out[P * m : P * (m + 1), n0 : n0 + width], in_=ob[:])
+
+        transposes(0)
+        transposes(1)
+        acc_a = [psum.tile([P, 512], F32, tag="bank%d" % m, name="accA%d" % m) for m in range(M_TILES)]
+        for c in range(N_CHUNKS):
+            quantise(c)
+            for gi in range(2):
+                for m in range(M_TILES):
+                    mx(acc_a[m][:], 2 * c + gi, m, wa[c][:, gi, :], pa, 0, 512)
+            if c + 2 < N_CHUNKS:
+                transposes(c + 2)
+        for m in range(M_TILES):
+            evacuate(acc_a[m][:], m, 0, 512, m % 2 == 0)
+
+        acc_b = [psum.tile([P, 512], F32, tag="bank%d" % (4 + m), name="accB%d" % m) for m in range(M_TILES)]
+        acc_c = [psum.tile([P, 512], F32, tag="bank%d" % m, name="accC%d" % m) for m in range(M_TILES)]
+        for g in range(PASSES):
+            for m in range(M_TILES):
+                mx(acc_b[m][:], g, m, wbc[g][:, 0:512], pr, 0, 512)
+            for m in range(M_TILES):
+                mx(acc_c[m][:], g, m, wbc[g][:, 512:1024], pr, 512, 512)
+        for m in range(M_TILES):
+            evacuate(acc_b[m][:], m, 512, 512, m % 2 == 0)
+        for m in range(M_TILES):
+            evacuate(acc_c[m][:], m, 1024, 512, m % 2 == 0)
+
+        for m in range(M_TILES):
+            acc_d = psum.tile([P, 256], F32, tag="bank%d" % (4 + m), name="accD%d" % m)
+            for g in range(PASSES):
+                mx(acc_d[:], g, m, wde[g // 5][:, g % 5, 0:256], pr, 1024, 256)
+            acc_e = psum.tile([P, 128], F32, tag="bank%d" % m, name="accE%d" % m)
+            for g in range(PASSES):
+                mx(acc_e[:], g, m, wde[g // 5][:, g % 5, 256:384], pr, 1280, 128)
+            evacuate(acc_d[:], m, 1536, 256, True)
+            evacuate(acc_e[:], m, 1792, 128, False)

@@ -9,6 +9,7 @@ F32 = mybir.dt.float32
 I32 = mybir.dt.int32
 U32 = mybir.dt.uint32
 U8 = mybir.dt.uint8
+ADD = mybir.AluOpType.add
 
 P = 128
 ROWS = 512
@@ -18,18 +19,18 @@ PASSES = 10
 M_TILES = 4
 FLOPS = 2 * ROWS * K * N_OUT
 
-N_CHUNKS = 5
-SORTED_FROM = 1
+N_NAT = 6
 
 
 def tile_applypolicymap_kernel(tc, x, fc1_words, fc1_scales, out):
     nc = tc.nc
     xf = x.rearrange("(m p) c h w -> p m (c h w)", p=P)
+    xc = x.rearrange("(c j) d h w -> j c (d h w)", j=32)
     ww = fc1_words.rearrange("g p n t -> g p (n t)").bitcast(I32).rearrange("g p n -> p g n")
+    chunks = [list(range(g, min(g + 2, N_NAT))) for g in range(0, N_NAT, 2)]
 
     with ExitStack() as ctx:
         const = ctx.enter_context(tc.tile_pool(name="const", bufs=1))
-        xs_pool = ctx.enter_context(tc.tile_pool(name="xs", bufs=4))
         xg_pool = ctx.enter_context(tc.tile_pool(name="xg", bufs=4))
         psum = ctx.enter_context(tc.psum_pool(name="psum", bufs=1))
         ctx.enter_context(tc.manual_schedule())
@@ -38,23 +39,31 @@ def tile_applypolicymap_kernel(tc, x, fc1_words, fc1_scales, out):
         warm_out = const.tile([P, 1], F32, name="warm_out")
         nc.vector.memset(warm_in[:], 0.0)
         nc.scalar.copy(out=warm_out[:], in_=warm_in[:])
-        pa = [const.tile([P, 512], U8, name="pa%d" % s, align_bytes=64) for s in range(3)]
-        pr = [const.tile([P, 1408], U8, name="pr%d" % s, align_bytes=64) for s in range(3)]
-        for t in pa + pr:
+        pl = [const.tile([P, 896], U8, name="pl%d" % s, align_bytes=64) for s in range(3)]
+        ph = [const.tile([P, 1024], U8, name="ph%d" % s, align_bytes=64) for s in range(3)]
+        for t in pl[0:2] + ph + pl[2:3]:
             nc.vector.memset(t[:].bitcast(I32), 0)
         ident = const.tile([P, P], F32, name="ident")
         make_identity(nc, ident[:])
 
         xr = {}
-        wa = []
-        wbc = []
-        wde = []
+        xin = {}
+        wl = {}
+        wab = {}
 
         def load_x(c):
+            gs = chunks[c]
             for j in range(2):
-                t = const.tile([P, 2, 1024], BF16, name="xr%d_%d" % (c, j))
-                nc.sync.dma_start(out=t[:], in_=xf[:, 2 * j : 2 * j + 2, 1024 * c : 1024 * (c + 1)])
+                t = const.tile([P, 2, 512 * len(gs)], BF16, name="xr%d_%d" % (c, j))
+                nc.sync.dma_start(out=t[:], in_=xf[:, 2 * j : 2 * j + 2, 512 * gs[0] : 512 * (gs[-1] + 1)])
                 xr[(c, j)] = t
+
+        def load_xin(g):
+            t = const.tile([P, 16, 128], BF16, name="xin%d" % g)
+            for a in range(4):
+                k0 = 512 * g + 128 * a
+                nc.sync.dma_start(out=t[32 * a : 32 * (a + 1), :, :], in_=xc[:, :, k0 : k0 + 128])
+            xin[g] = t
 
         def load_planes(tiles, s, c0, c1):
             n_planes = min(4, PASSES - 4 * s)
@@ -64,80 +73,51 @@ def tile_applypolicymap_kernel(tc, x, fc1_words, fc1_scales, out):
                     in_=fc1_scales[4 * s : 4 * s + n_planes, 4 * q : 4 * q + 4, c0:c1].bitcast(I32),
                 )
 
-        def load_wa(c):
-            t = const.tile([P, 2, 512], U32, name="wa%d" % c, align_bytes=64)
-            nc.sync.dma_start(out=t[:].bitcast(I32), in_=ww[:, 2 * c : 2 * c + 2, 0:512])
-            wa.append(t)
+        def load_wl(g):
+            t = const.tile([P, 896], U32, name="wl%d" % g, align_bytes=64)
+            nc.sync.dma_start(out=t[:].bitcast(I32), in_=ww[:, g, 1024:1920])
+            wl[g] = t
 
-        def load_wbc(g):
-            t = const.tile([P, 1024], U32, name="wbc%d" % g, align_bytes=64)
-            nc.sync.dma_start(out=t[:].bitcast(I32), in_=ww[:, g, 512:1536])
-            wbc.append(t)
+        def load_wab(g):
+            t = const.tile([P, 1024], U32, name="wab%d" % g, align_bytes=64)
+            nc.sync.dma_start(out=t[:].bitcast(I32), in_=ww[:, g, 0:1024])
+            wab[g] = t
 
-        def load_wde(h):
-            t = const.tile([P, 5, 384], U32, name="wde%d" % h, align_bytes=64)
-            nc.sync.dma_start(out=t[:].bitcast(I32), in_=ww[:, 5 * h : 5 * h + 5, 1536:1920])
-            wde.append(t)
-
-        load_x(0)
-        load_x(1)
-        load_planes(pa, 0, 0, 512)
-        load_wa(0)
-        load_x(2)
-        load_planes(pa, 1, 0, 512)
-        load_wa(1)
-        load_x(3)
-        load_wa(2)
-        load_x(4)
-        load_planes(pa, 2, 0, 512)
-        load_wa(3)
-        load_wa(4)
-        load_planes(pr, 0, 512, 1920)
-        for g in range(0, 4):
-            load_wbc(g)
-        load_planes(pr, 1, 512, 1920)
-        load_planes(pr, 2, 512, 1920)
-        for g in range(4, PASSES):
-            load_wbc(g)
-        load_wde(0)
-        load_wde(1)
+        for c in range(len(chunks)):
+            load_x(c)
+        load_planes(pl, 0, 1024, 1920)
+        load_wl(0)
+        load_planes(pl, 1, 1024, 1920)
+        for g in range(1, N_NAT):
+            load_wl(g)
+        load_planes(ph, 0, 0, 1024)
+        load_xin(N_NAT)
+        load_wab(0)
+        load_wab(1)
+        load_planes(ph, 1, 0, 1024)
+        load_planes(ph, 2, 0, 1024)
+        load_planes(pl, 2, 1024, 1920)
+        next_wab = 2
+        for g in range(N_NAT + 1, PASSES):
+            load_xin(g)
+            load_wab(next_wab)
+            load_wab(next_wab + 1)
+            next_wab += 2
+        for g in range(next_wab, PASSES):
+            load_wab(g)
+        for g in range(N_NAT, PASSES):
+            load_wl(g)
 
         xg = {}
         xq = {}
         xp = {}
 
-        def transposes(c):
-            for gi in range(2):
-                g = 2 * c + gi
-                xg[g] = xg_pool.tile([P, 2048], BF16, tag="xg", name="xg%d" % g, align_bytes=64)
-            for j in range(2):
-                xw = xr[(c, j)][:].rearrange("p m k -> p (m k)").bitcast(F32)
-                if c >= SORTED_FROM:
-                    xs = xs_pool.tile([P, 4, 2, P], F32, tag="xs", name="xs%d_%d" % (c, j))
-                    nc.vector.tensor_copy(out=xs[:], in_=xw.rearrange("p (a q u) -> p a u q", a=4, q=P, u=2))
-                for gi in range(2):
-                    g = 2 * c + gi
-                    bank = 2 * j + gi if c == 0 else 4 + 2 * j + gi
-                    tb = psum.tile([P, 2, 2, P], F32, tag="bank%d" % bank, name="tb%d_%d" % (g, j))
-                    for mi in range(2):
-                        a = 2 * mi + gi
-                        for u in range(2):
-                            if c >= SORTED_FROM:
-                                src = xs[:, a, u, :]
-                            else:
-                                src = xw[:, 256 * a + u : 256 * (a + 1) : 2]
-                            nc.tensor.transpose(tb[:, mi, u, :], src, ident[:])
-                    dst = xg[g][:].bitcast(F32).rearrange("p (m r u) -> p m r u", m=4, r=P, u=2)
-                    nc.scalar.copy(out=dst[:, 2 * j : 2 * j + 2], in_=tb[:].rearrange("p m u r -> p m r u"))
+        def quantise(g):
+            xq[g] = const.tile([P, ROWS], U32, name="xq%d" % g, align_bytes=64)
+            xp[g] = const.tile([P, ROWS], U8, name="xp%d" % g, align_bytes=64)
+            nc.vector.quantize_mx(out=xq[g][:].bitcast(FP8X4), scales=xp[g][:], in_=xg[g][:])
 
-        def quantise(c):
-            for gi in range(2):
-                g = 2 * c + gi
-                xq[g] = const.tile([P, ROWS], U32, name="xq%d" % g, align_bytes=64)
-                xp[g] = const.tile([P, ROWS], U8, name="xp%d" % g, align_bytes=64)
-                nc.vector.quantize_mx(out=xq[g][:].bitcast(FP8X4), scales=xp[g][:], in_=xg[g][:])
-
-        def mx(acc, g, m, rhs, planes, col0, width):
+        def mx(acc, g, m, rhs, planes, col0, width, first, last):
             k = 4 * (g % 4)
             nc.tensor.matmul_mx(
                 out=acc,
@@ -145,49 +125,109 @@ def tile_applypolicymap_kernel(tc, x, fc1_words, fc1_scales, out):
                 lhsT_scale=xp[g][:, P * m : P * (m + 1)],
                 rhs=rhs.bitcast(FP8X4),
                 rhs_scale=planes[g // 4][k:P, col0 : col0 + width],
-                start=(g == 0),
-                stop=(g == PASSES - 1),
+                start=first,
+                stop=last,
             )
 
-        def evacuate(acc, m, n0, width, on_scalar):
-            ob = const.tile([P, width], F32, name="ob%d_%d" % (m, n0))
-            if on_scalar:
-                nc.scalar.copy(out=ob[:], in_=acc)
+        def store(src, m, n0, width):
+            nc.sync.dma_start(out=out[P * m : P * (m + 1), n0 : n0 + width], in_=src)
+
+        for c in range(len(chunks)):
+            gs = chunks[c]
+            ng = len(gs)
+            for g in gs:
+                xg[g] = xg_pool.tile([P, 2048], BF16, tag="xg", name="xg%d" % g, align_bytes=64)
+            for j in range(2):
+                xw = xr[(c, j)][:].rearrange("p m k -> p (m k)").bitcast(F32)
+                for gi in range(ng):
+                    g = gs[gi]
+                    fill = 4 * c + ng * j + gi
+                    tb = psum.tile([P, 2, 2, P], F32, tag="bank%d" % (fill % 8), name="tb%d_%d" % (g, j))
+                    for mi in range(2):
+                        w0 = 256 * (mi * ng + gi)
+                        for u in range(2):
+                            nc.tensor.transpose(tb[:, mi, u, :], xw[:, w0 + u : w0 + 256 : 2], ident[:])
+                    dst = xg[g][:].bitcast(F32).rearrange("p (m r u) -> p m r u", m=4, r=P, u=2)
+                    if fill % 2 == 0:
+                        nc.scalar.copy(out=dst[:, 2 * j : 2 * j + 2], in_=tb[:].rearrange("p m u r -> p m r u"))
+                    else:
+                        nc.vector.tensor_copy(out=dst[:, 2 * j : 2 * j + 2], in_=tb[:].rearrange("p m u r -> p m r u"))
+            for g in gs:
+                quantise(g)
+
+        for g in range(N_NAT, PASSES):
+            xw = xin[g][:].rearrange("p c k -> p (c k)").bitcast(F32)
+            so = const.tile([P, 1024], F32, tag="so", name="so%d" % g, align_bytes=64)
+            nc.vector.tensor_copy(
+                out=so[:].rearrange("p (c u i) -> p c u i", c=16, u=2, i=32),
+                in_=xw.rearrange("p (c i u) -> p c u i", c=16, i=32, u=2),
+            )
+            vt = const.tile([P, 1024], F32, tag="vt", name="vt%d" % g, align_bytes=64)
+            nc.vector.transpose(out=vt[:], in_=so[:])
+            xg[g] = xg_pool.tile([P, 2048], BF16, tag="xg", name="xg%d" % g, align_bytes=64)
+            nc.vector.tensor_copy(
+                out=xg[g][:].bitcast(F32).rearrange("p (c j u) -> p c j u", c=16, j=32, u=2),
+                in_=vt[:].rearrange("p (c u j) -> p c j u", c=16, u=2, j=32),
+            )
+            quantise(g)
+
+        acc_c = [psum.tile([P, 512], F32, tag="bank%d" % (4 + m), name="accC%d" % m) for m in range(M_TILES)]
+        acc_de = [psum.tile([P, 384], F32, tag="bank%d" % m, name="accDE%d" % m) for m in range(M_TILES)]
+        for g in range(N_NAT):
+            for m in range(M_TILES):
+                mx(acc_c[m][:], g, m, wl[g][:, 0:512], pl, 0, 512, g == 0, g == N_NAT - 1)
+            for m in range(M_TILES):
+                mx(acc_de[m][:, 0:256], g, m, wl[g][:, 512:768], pl, 512, 256, g == 0, g == N_NAT - 1)
+        pc = []
+        pde = []
+        for m in range(M_TILES):
+            t = const.tile([P, 512], F32, name="pc%d" % m)
+            nc.scalar.copy(out=t[:], in_=acc_c[m][:])
+            pc.append(t)
+        for m in range(M_TILES):
+            for g in range(N_NAT):
+                mx(acc_de[m][:, 256:384], g, m, wl[g][:, 768:896], pl, 768, 128, g == 0, g == N_NAT - 1)
+        for m in range(M_TILES):
+            t = const.tile([P, 384], F32, name="pde%d" % m)
+            nc.scalar.copy(out=t[:], in_=acc_de[m][:])
+            pde.append(t)
+
+        acc_a = [psum.tile([P, 512], F32, tag="bank%d" % (4 + m), name="accA%d" % m) for m in range(M_TILES)]
+        acc_b = [psum.tile([P, 512], F32, tag="bank%d" % m, name="accB%d" % m) for m in range(M_TILES)]
+        for g0 in range(0, PASSES, 2):
+            for acc, c0 in ((acc_a, 0), (acc_b, 512)):
+                for g in (g0, g0 + 1):
+                    for m in range(M_TILES):
+                        mx(acc[m][:], g, m, wab[g][:, c0 : c0 + 512], ph, c0, 512, g == 0, g == PASSES - 1)
+        for acc, c0 in ((acc_a, 0), (acc_b, 512)):
+            for m in range(M_TILES):
+                t = const.tile([P, 512], F32, name="oab%d_%d" % (m, c0))
+                nc.scalar.copy(out=t[:], in_=acc[m][:])
+                store(t[:], m, c0, 512)
+
+        def finish(acc, part, m, n0, width):
+            t = const.tile([P, width], F32, name="o%d_%d" % (m, n0))
+            nc.vector.tensor_tensor(out=t[:], in0=acc, in1=part, op=ADD)
+            store(t[:], m, n0, width)
+
+        for m in range(M_TILES):
+            c2 = psum.tile([P, 512], F32, tag="bank%d" % (4 + m), name="c2_%d" % m)
+            for g in range(N_NAT, PASSES):
+                mx(c2[:], g, m, wl[g][:, 0:512], pl, 0, 512, g == N_NAT, g == PASSES - 1)
+            finish(c2[:], pc[m][:], m, 1024, 512)
+            if m < M_TILES - 1:
+                de2 = psum.tile([P, 384], F32, tag="bank%d" % m, name="de2_%d" % m)
+                for g in range(N_NAT, PASSES):
+                    mx(de2[:, 0:256], g, m, wl[g][:, 512:768], pl, 512, 256, g == N_NAT, g == PASSES - 1)
+                for g in range(N_NAT, PASSES):
+                    mx(de2[:, 256:384], g, m, wl[g][:, 768:896], pl, 768, 128, g == N_NAT, g == PASSES - 1)
+                finish(de2[:], pde[m][:], m, 1536, 384)
             else:
-                nc.vector.tensor_copy(out=ob[:], in_=acc)
-            nc.sync.dma_start(out=out[P * m : P * (m + 1), n0 : n0 + width], in_=ob[:])
-
-        transposes(0)
-        transposes(1)
-        acc_a = [psum.tile([P, 512], F32, tag="bank%d" % m, name="accA%d" % m) for m in range(M_TILES)]
-        for c in range(N_CHUNKS):
-            quantise(c)
-            for gi in range(2):
-                for m in range(M_TILES):
-                    mx(acc_a[m][:], 2 * c + gi, m, wa[c][:, gi, :], pa, 0, 512)
-            if c + 2 < N_CHUNKS:
-                transposes(c + 2)
-        for m in range(M_TILES):
-            evacuate(acc_a[m][:], m, 0, 512, m % 2 == 0)
-
-        acc_b = [psum.tile([P, 512], F32, tag="bank%d" % (4 + m), name="accB%d" % m) for m in range(M_TILES)]
-        acc_c = [psum.tile([P, 512], F32, tag="bank%d" % m, name="accC%d" % m) for m in range(M_TILES)]
-        for g in range(PASSES):
-            for m in range(M_TILES):
-                mx(acc_b[m][:], g, m, wbc[g][:, 0:512], pr, 0, 512)
-            for m in range(M_TILES):
-                mx(acc_c[m][:], g, m, wbc[g][:, 512:1024], pr, 512, 512)
-        for m in range(M_TILES):
-            evacuate(acc_b[m][:], m, 512, 512, m % 2 == 0)
-        for m in range(M_TILES):
-            evacuate(acc_c[m][:], m, 1024, 512, m % 2 == 0)
-
-        for m in range(M_TILES):
-            acc_d = psum.tile([P, 256], F32, tag="bank%d" % (4 + m), name="accD%d" % m)
-            for g in range(PASSES):
-                mx(acc_d[:], g, m, wde[g // 5][:, g % 5, 0:256], pr, 1024, 256)
-            acc_e = psum.tile([P, 128], F32, tag="bank%d" % m, name="accE%d" % m)
-            for g in range(PASSES):
-                mx(acc_e[:], g, m, wde[g // 5][:, g % 5, 256:384], pr, 1280, 128)
-            evacuate(acc_d[:], m, 1536, 256, True)
-            evacuate(acc_e[:], m, 1792, 128, False)
+                d2 = psum.tile([P, 256], F32, tag="bank%d" % m, name="d2_%d" % m)
+                for g in range(N_NAT, PASSES):
+                    mx(d2[:], g, m, wl[g][:, 512:768], pl, 512, 256, g == N_NAT, g == PASSES - 1)
+                finish(d2[:], pde[m][:, 0:256], m, 1536, 256)
+                e2 = psum.tile([P, 128], F32, tag="bank0", name="e2_%d" % m)
+                for g in range(N_NAT, PASSES):
+                    mx(e2[:], g, m, wl[g][:, 768:896], pl, 768, 128, g == N_NAT, g == PASSES - 1)
+                finish(e2[:], pde[m][:, 256:384], m, 1792, 128)

@@ -9,7 +9,6 @@ F32 = mybir.dt.float32
 I32 = mybir.dt.int32
 U32 = mybir.dt.uint32
 U8 = mybir.dt.uint8
-ADD = mybir.AluOpType.add
 
 P = 128
 ROWS = 512
@@ -19,18 +18,18 @@ PASSES = 10
 M_TILES = 4
 FLOPS = 2 * ROWS * K * N_OUT
 
-N_NAT = 6
+N_CHUNKS = 5
+SORTED_FROM = 2
 
 
 def tile_applypolicymap_kernel(tc, x, fc1_words, fc1_scales, out):
     nc = tc.nc
     xf = x.rearrange("(m p) c h w -> p m (c h w)", p=P)
-    xc = x.rearrange("(c j) d h w -> j c (d h w)", j=32)
     ww = fc1_words.rearrange("g p n t -> g p (n t)").bitcast(I32).rearrange("g p n -> p g n")
-    chunks = [list(range(g, min(g + 2, N_NAT))) for g in range(0, N_NAT, 2)]
 
     with ExitStack() as ctx:
         const = ctx.enter_context(tc.tile_pool(name="const", bufs=1))
+        xs_pool = ctx.enter_context(tc.tile_pool(name="xs", bufs=4))
         xg_pool = ctx.enter_context(tc.tile_pool(name="xg", bufs=4))
         psum = ctx.enter_context(tc.psum_pool(name="psum", bufs=1))
         ctx.enter_context(tc.manual_schedule())
@@ -39,31 +38,23 @@ def tile_applypolicymap_kernel(tc, x, fc1_words, fc1_scales, out):
         warm_out = const.tile([P, 1], F32, name="warm_out")
         nc.vector.memset(warm_in[:], 0.0)
         nc.scalar.copy(out=warm_out[:], in_=warm_in[:])
-        pl = [const.tile([P, 896], U8, name="pl%d" % s, align_bytes=64) for s in range(3)]
-        ph = [const.tile([P, 1024], U8, name="ph%d" % s, align_bytes=64) for s in range(3)]
-        for t in pl[0:2] + ph + pl[2:3]:
+        pa = [const.tile([P, 512], U8, name="pa%d" % s, align_bytes=64) for s in range(3)]
+        pr = [const.tile([P, 1408], U8, name="pr%d" % s, align_bytes=64) for s in range(3)]
+        for t in pa + pr:
             nc.vector.memset(t[:].bitcast(I32), 0)
         ident = const.tile([P, P], F32, name="ident")
         make_identity(nc, ident[:])
 
         xr = {}
-        xin = {}
-        wl = {}
-        wab = {}
+        wa = []
+        wbc = []
+        wde = []
 
         def load_x(c):
-            gs = chunks[c]
             for j in range(2):
-                t = const.tile([P, 2, 512 * len(gs)], BF16, name="xr%d_%d" % (c, j))
-                nc.sync.dma_start(out=t[:], in_=xf[:, 2 * j : 2 * j + 2, 512 * gs[0] : 512 * (gs[-1] + 1)])
+                t = const.tile([P, 2, 1024], BF16, name="xr%d_%d" % (c, j))
+                nc.sync.dma_start(out=t[:], in_=xf[:, 2 * j : 2 * j + 2, 1024 * c : 1024 * (c + 1)])
                 xr[(c, j)] = t
-
-        def load_xin(g):
-            t = const.tile([P, 16, 128], BF16, name="xin%d" % g)
-            for a in range(4):
-                k0 = 512 * g + 128 * a
-                nc.sync.dma_start(out=t[32 * a : 32 * (a + 1), :, :], in_=xc[:, :, k0 : k0 + 128])
-            xin[g] = t
 
         def load_planes(tiles, s, c0, c1):
             n_planes = min(4, PASSES - 4 * s)
@@ -73,51 +64,87 @@ def tile_applypolicymap_kernel(tc, x, fc1_words, fc1_scales, out):
                     in_=fc1_scales[4 * s : 4 * s + n_planes, 4 * q : 4 * q + 4, c0:c1].bitcast(I32),
                 )
 
-        def load_wl(g):
-            t = const.tile([P, 896], U32, name="wl%d" % g, align_bytes=64)
-            nc.sync.dma_start(out=t[:].bitcast(I32), in_=ww[:, g, 1024:1920])
-            wl[g] = t
+        def load_wa(c):
+            if c == 0:
+                for g in range(2):
+                    t = const.tile([P, 512], U32, name="wa0_%d" % g, align_bytes=64)
+                    nc.sync.dma_start(out=t[:].bitcast(I32), in_=ww[:, g, 0:512])
+                    wa.append(t[:])
+            else:
+                t = const.tile([P, 2, 512], U32, name="wa%d" % c, align_bytes=64)
+                nc.sync.dma_start(out=t[:].bitcast(I32), in_=ww[:, 2 * c : 2 * c + 2, 0:512])
+                wa.append(t[:, 0, :])
+                wa.append(t[:, 1, :])
 
-        def load_wab(g):
-            t = const.tile([P, 1024], U32, name="wab%d" % g, align_bytes=64)
-            nc.sync.dma_start(out=t[:].bitcast(I32), in_=ww[:, g, 0:1024])
-            wab[g] = t
+        def load_wbc(g):
+            t = const.tile([P, 1024], U32, name="wbc%d" % g, align_bytes=64)
+            nc.sync.dma_start(out=t[:].bitcast(I32), in_=ww[:, g, 512:1536])
+            wbc.append(t)
 
-        for c in range(len(chunks)):
-            load_x(c)
-        load_planes(pl, 0, 1024, 1920)
-        load_wl(0)
-        load_planes(pl, 1, 1024, 1920)
-        for g in range(1, N_NAT):
-            load_wl(g)
-        load_planes(ph, 0, 0, 1024)
-        load_xin(N_NAT)
-        load_wab(0)
-        load_wab(1)
-        load_planes(ph, 1, 0, 1024)
-        load_planes(ph, 2, 0, 1024)
-        load_planes(pl, 2, 1024, 1920)
-        next_wab = 2
-        for g in range(N_NAT + 1, PASSES):
-            load_xin(g)
-            load_wab(next_wab)
-            load_wab(next_wab + 1)
-            next_wab += 2
-        for g in range(next_wab, PASSES):
-            load_wab(g)
-        for g in range(N_NAT, PASSES):
-            load_wl(g)
+        def load_wde(h):
+            t = const.tile([P, 5, 384], U32, name="wde%d" % h, align_bytes=64)
+            nc.sync.dma_start(out=t[:].bitcast(I32), in_=ww[:, 5 * h : 5 * h + 5, 1536:1920])
+            wde.append(t)
+
+        load_x(0)
+        load_x(1)
+        load_planes(pa, 0, 0, 512)
+        load_wa(0)
+        load_x(2)
+        load_planes(pa, 1, 0, 512)
+        load_wa(1)
+        load_x(3)
+        load_wa(2)
+        load_x(4)
+        load_planes(pa, 2, 0, 512)
+        load_wa(3)
+        load_wa(4)
+        load_planes(pr, 0, 512, 1920)
+        for g in range(0, 4):
+            load_wbc(g)
+        load_planes(pr, 1, 512, 1920)
+        load_planes(pr, 2, 512, 1920)
+        for g in range(4, PASSES):
+            load_wbc(g)
+        load_wde(0)
+        load_wde(1)
 
         xg = {}
         xq = {}
         xp = {}
 
-        def quantise(g):
-            xq[g] = const.tile([P, ROWS], U32, name="xq%d" % g, align_bytes=64)
-            xp[g] = const.tile([P, ROWS], U8, name="xp%d" % g, align_bytes=64)
-            nc.vector.quantize_mx(out=xq[g][:].bitcast(FP8X4), scales=xp[g][:], in_=xg[g][:])
+        def transposes(c):
+            for gi in range(2):
+                g = 2 * c + gi
+                xg[g] = xg_pool.tile([P, 2048], BF16, tag="xg", name="xg%d" % g, align_bytes=64)
+            for j in range(2):
+                xw = xr[(c, j)][:].rearrange("p m k -> p (m k)").bitcast(F32)
+                if c >= SORTED_FROM:
+                    xs = xs_pool.tile([P, 4, 2, P], F32, tag="xs", name="xs%d_%d" % (c, j))
+                    nc.vector.tensor_copy(out=xs[:], in_=xw.rearrange("p (a q u) -> p a u q", a=4, q=P, u=2))
+                for gi in range(2):
+                    g = 2 * c + gi
+                    bank = 2 * j + gi if c == 0 else 4 + 2 * j + gi
+                    tb = psum.tile([P, 2, 2, P], F32, tag="bank%d" % bank, name="tb%d_%d" % (g, j))
+                    for mi in range(2):
+                        a = 2 * mi + gi
+                        for u in range(2):
+                            if c >= SORTED_FROM:
+                                src = xs[:, a, u, :]
+                            else:
+                                src = xw[:, 256 * a + u : 256 * (a + 1) : 2]
+                            nc.tensor.transpose(tb[:, mi, u, :], src, ident[:])
+                    dst = xg[g][:].bitcast(F32).rearrange("p (m r u) -> p m r u", m=4, r=P, u=2)
+                    nc.scalar.copy(out=dst[:, 2 * j : 2 * j + 2], in_=tb[:].rearrange("p m u r -> p m r u"))
 
-        def mx(acc, g, m, rhs, planes, col0, width, first, last):
+        def quantise(c):
+            for gi in range(2):
+                g = 2 * c + gi
+                xq[g] = const.tile([P, ROWS], U32, name="xq%d" % g, align_bytes=64)
+                xp[g] = const.tile([P, ROWS], U8, name="xp%d" % g, align_bytes=64)
+                nc.vector.quantize_mx(out=xq[g][:].bitcast(FP8X4), scales=xp[g][:], in_=xg[g][:])
+
+        def mx(acc, g, m, rhs, planes, col0, width):
             k = 4 * (g % 4)
             nc.tensor.matmul_mx(
                 out=acc,
@@ -125,109 +152,49 @@ def tile_applypolicymap_kernel(tc, x, fc1_words, fc1_scales, out):
                 lhsT_scale=xp[g][:, P * m : P * (m + 1)],
                 rhs=rhs.bitcast(FP8X4),
                 rhs_scale=planes[g // 4][k:P, col0 : col0 + width],
-                start=first,
-                stop=last,
+                start=(g == 0),
+                stop=(g == PASSES - 1),
             )
 
-        def store(src, m, n0, width):
-            nc.sync.dma_start(out=out[P * m : P * (m + 1), n0 : n0 + width], in_=src)
-
-        for c in range(len(chunks)):
-            gs = chunks[c]
-            ng = len(gs)
-            for g in gs:
-                xg[g] = xg_pool.tile([P, 2048], BF16, tag="xg", name="xg%d" % g, align_bytes=64)
-            for j in range(2):
-                xw = xr[(c, j)][:].rearrange("p m k -> p (m k)").bitcast(F32)
-                for gi in range(ng):
-                    g = gs[gi]
-                    fill = 4 * c + ng * j + gi
-                    tb = psum.tile([P, 2, 2, P], F32, tag="bank%d" % (fill % 8), name="tb%d_%d" % (g, j))
-                    for mi in range(2):
-                        w0 = 256 * (mi * ng + gi)
-                        for u in range(2):
-                            nc.tensor.transpose(tb[:, mi, u, :], xw[:, w0 + u : w0 + 256 : 2], ident[:])
-                    dst = xg[g][:].bitcast(F32).rearrange("p (m r u) -> p m r u", m=4, r=P, u=2)
-                    if fill % 2 == 0:
-                        nc.scalar.copy(out=dst[:, 2 * j : 2 * j + 2], in_=tb[:].rearrange("p m u r -> p m r u"))
-                    else:
-                        nc.vector.tensor_copy(out=dst[:, 2 * j : 2 * j + 2], in_=tb[:].rearrange("p m u r -> p m r u"))
-            for g in gs:
-                quantise(g)
-
-        for g in range(N_NAT, PASSES):
-            xw = xin[g][:].rearrange("p c k -> p (c k)").bitcast(F32)
-            so = const.tile([P, 1024], F32, tag="so", name="so%d" % g, align_bytes=64)
-            nc.vector.tensor_copy(
-                out=so[:].rearrange("p (c u i) -> p c u i", c=16, u=2, i=32),
-                in_=xw.rearrange("p (c i u) -> p c u i", c=16, i=32, u=2),
-            )
-            vt = const.tile([P, 1024], F32, tag="vt", name="vt%d" % g, align_bytes=64)
-            nc.vector.transpose(out=vt[:], in_=so[:])
-            xg[g] = xg_pool.tile([P, 2048], BF16, tag="xg", name="xg%d" % g, align_bytes=64)
-            nc.vector.tensor_copy(
-                out=xg[g][:].bitcast(F32).rearrange("p (c j u) -> p c j u", c=16, j=32, u=2),
-                in_=vt[:].rearrange("p (c u j) -> p c j u", c=16, u=2, j=32),
-            )
-            quantise(g)
-
-        acc_c = [psum.tile([P, 512], F32, tag="bank%d" % (4 + m), name="accC%d" % m) for m in range(M_TILES)]
-        acc_de = [psum.tile([P, 384], F32, tag="bank%d" % m, name="accDE%d" % m) for m in range(M_TILES)]
-        for g in range(N_NAT):
-            for m in range(M_TILES):
-                mx(acc_c[m][:], g, m, wl[g][:, 0:512], pl, 0, 512, g == 0, g == N_NAT - 1)
-            for m in range(M_TILES):
-                mx(acc_de[m][:, 0:256], g, m, wl[g][:, 512:768], pl, 512, 256, g == 0, g == N_NAT - 1)
-        pc = []
-        pde = []
-        for m in range(M_TILES):
-            t = const.tile([P, 512], F32, name="pc%d" % m)
-            nc.scalar.copy(out=t[:], in_=acc_c[m][:])
-            pc.append(t)
-        for m in range(M_TILES):
-            for g in range(N_NAT):
-                mx(acc_de[m][:, 256:384], g, m, wl[g][:, 768:896], pl, 768, 128, g == 0, g == N_NAT - 1)
-        for m in range(M_TILES):
-            t = const.tile([P, 384], F32, name="pde%d" % m)
-            nc.scalar.copy(out=t[:], in_=acc_de[m][:])
-            pde.append(t)
-
-        acc_a = [psum.tile([P, 512], F32, tag="bank%d" % (4 + m), name="accA%d" % m) for m in range(M_TILES)]
-        acc_b = [psum.tile([P, 512], F32, tag="bank%d" % m, name="accB%d" % m) for m in range(M_TILES)]
-        for g0 in range(0, PASSES, 2):
-            for acc, c0 in ((acc_a, 0), (acc_b, 512)):
-                for g in (g0, g0 + 1):
-                    for m in range(M_TILES):
-                        mx(acc[m][:], g, m, wab[g][:, c0 : c0 + 512], ph, c0, 512, g == 0, g == PASSES - 1)
-        for acc, c0 in ((acc_a, 0), (acc_b, 512)):
-            for m in range(M_TILES):
-                t = const.tile([P, 512], F32, name="oab%d_%d" % (m, c0))
-                nc.scalar.copy(out=t[:], in_=acc[m][:])
-                store(t[:], m, c0, 512)
-
-        def finish(acc, part, m, n0, width):
-            t = const.tile([P, width], F32, name="o%d_%d" % (m, n0))
-            nc.vector.tensor_tensor(out=t[:], in0=acc, in1=part, op=ADD)
-            store(t[:], m, n0, width)
-
-        for m in range(M_TILES):
-            c2 = psum.tile([P, 512], F32, tag="bank%d" % (4 + m), name="c2_%d" % m)
-            for g in range(N_NAT, PASSES):
-                mx(c2[:], g, m, wl[g][:, 0:512], pl, 0, 512, g == N_NAT, g == PASSES - 1)
-            finish(c2[:], pc[m][:], m, 1024, 512)
-            if m < M_TILES - 1:
-                de2 = psum.tile([P, 384], F32, tag="bank%d" % m, name="de2_%d" % m)
-                for g in range(N_NAT, PASSES):
-                    mx(de2[:, 0:256], g, m, wl[g][:, 512:768], pl, 512, 256, g == N_NAT, g == PASSES - 1)
-                for g in range(N_NAT, PASSES):
-                    mx(de2[:, 256:384], g, m, wl[g][:, 768:896], pl, 768, 128, g == N_NAT, g == PASSES - 1)
-                finish(de2[:], pde[m][:], m, 1536, 384)
+        def evacuate(acc, m, n0, width, on_scalar):
+            ob = const.tile([P, width], F32, name="ob%d_%d" % (m, n0))
+            if on_scalar:
+                nc.scalar.copy(out=ob[:], in_=acc)
             else:
-                d2 = psum.tile([P, 256], F32, tag="bank%d" % m, name="d2_%d" % m)
-                for g in range(N_NAT, PASSES):
-                    mx(d2[:], g, m, wl[g][:, 512:768], pl, 512, 256, g == N_NAT, g == PASSES - 1)
-                finish(d2[:], pde[m][:, 0:256], m, 1536, 256)
-                e2 = psum.tile([P, 128], F32, tag="bank0", name="e2_%d" % m)
-                for g in range(N_NAT, PASSES):
-                    mx(e2[:], g, m, wl[g][:, 768:896], pl, 768, 128, g == N_NAT, g == PASSES - 1)
-                finish(e2[:], pde[m][:, 256:384], m, 1792, 128)
+                nc.vector.tensor_copy(out=ob[:], in_=acc)
+            nc.sync.dma_start(out=out[P * m : P * (m + 1), n0 : n0 + width], in_=ob[:])
+
+        transposes(0)
+        transposes(1)
+        acc_a = [psum.tile([P, 512], F32, tag="bank%d" % m, name="accA%d" % m) for m in range(M_TILES)]
+        for c in range(N_CHUNKS):
+            quantise(c)
+            for gi in range(2):
+                for m in range(M_TILES):
+                    mx(acc_a[m][:], 2 * c + gi, m, wa[2 * c + gi], pa, 0, 512)
+            if c + 2 < N_CHUNKS:
+                transposes(c + 2)
+        for m in range(M_TILES):
+            evacuate(acc_a[m][:], m, 0, 512, m % 2 == 0)
+
+        acc_b = [psum.tile([P, 512], F32, tag="bank%d" % (4 + m), name="accB%d" % m) for m in range(M_TILES)]
+        acc_c = [psum.tile([P, 512], F32, tag="bank%d" % m, name="accC%d" % m) for m in range(M_TILES)]
+        for g in range(PASSES):
+            for m in range(M_TILES):
+                mx(acc_b[m][:], g, m, wbc[g][:, 0:512], pr, 0, 512)
+            for m in range(M_TILES):
+                mx(acc_c[m][:], g, m, wbc[g][:, 512:1024], pr, 512, 512)
+        for m in range(M_TILES):
+            evacuate(acc_b[m][:], m, 512, 512, m % 2 == 0)
+        for m in range(M_TILES):
+            evacuate(acc_c[m][:], m, 1024, 512, m % 2 == 0)
+
+        for m in range(M_TILES):
+            acc_d = psum.tile([P, 256], F32, tag="bank%d" % (4 + m), name="accD%d" % m)
+            for g in range(PASSES):
+                mx(acc_d[:], g, m, wde[g // 5][:, g % 5, 0:256], pr, 1024, 256)
+            acc_e = psum.tile([P, 128], F32, tag="bank%d" % m, name="accE%d" % m)
+            for g in range(PASSES):
+                mx(acc_e[:], g, m, wde[g // 5][:, g % 5, 256:384], pr, 1280, 128)
+            evacuate(acc_d[:], m, 1536, 256, True)
+            evacuate(acc_e[:], m, 1792, 128, False)

@@ -9,6 +9,7 @@ F32 = mybir.dt.float32
 I32 = mybir.dt.int32
 U32 = mybir.dt.uint32
 U8 = mybir.dt.uint8
+ADD = mybir.AluOpType.add
 
 P = 128
 ROWS = 512
@@ -31,6 +32,7 @@ def tile_applypolicymap_kernel(tc, x, fc1_words, fc1_scales, out):
         const = ctx.enter_context(tc.tile_pool(name="const", bufs=1))
         xs_pool = ctx.enter_context(tc.tile_pool(name="xs", bufs=4))
         xg_pool = ctx.enter_context(tc.tile_pool(name="xg", bufs=4))
+        pb_pool = ctx.enter_context(tc.tile_pool(name="pb", bufs=2))
         psum = ctx.enter_context(tc.psum_pool(name="psum", bufs=1))
         ctx.enter_context(tc.manual_schedule())
 
@@ -38,17 +40,16 @@ def tile_applypolicymap_kernel(tc, x, fc1_words, fc1_scales, out):
         warm_out = const.tile([P, 1], F32, name="warm_out")
         nc.vector.memset(warm_in[:], 0.0)
         nc.scalar.copy(out=warm_out[:], in_=warm_in[:])
-        pa = [const.tile([P, 512], U8, name="pa%d" % s, align_bytes=64) for s in range(3)]
-        pr = [const.tile([P, 1408], U8, name="pr%d" % s, align_bytes=64) for s in range(3)]
-        for t in pa + pr:
+        ph = [const.tile([P, 1024], U8, name="ph%d" % s, align_bytes=64) for s in range(3)]
+        pl = [const.tile([P, 896], U8, name="pl%d" % s, align_bytes=64) for s in range(3)]
+        for t in ph + pl:
             nc.vector.memset(t[:].bitcast(I32), 0)
         ident = const.tile([P, P], F32, name="ident")
         make_identity(nc, ident[:])
 
         xr = {}
-        wa = []
-        wbc = []
-        wde = []
+        wl = {}
+        wab = {}
 
         def load_x(c):
             for j in range(2):
@@ -64,64 +65,61 @@ def tile_applypolicymap_kernel(tc, x, fc1_words, fc1_scales, out):
                     in_=fc1_scales[4 * s : 4 * s + n_planes, 4 * q : 4 * q + 4, c0:c1].bitcast(I32),
                 )
 
-        def load_wa(c):
-            if c == 0:
-                for g in range(2):
-                    t = const.tile([P, 512], U32, name="wa0_%d" % g, align_bytes=64)
-                    nc.sync.dma_start(out=t[:].bitcast(I32), in_=ww[:, g, 0:512])
-                    wa.append(t[:])
-            else:
-                t = const.tile([P, 2, 512], U32, name="wa%d" % c, align_bytes=64)
-                nc.sync.dma_start(out=t[:].bitcast(I32), in_=ww[:, 2 * c : 2 * c + 2, 0:512])
-                wa.append(t[:, 0, :])
-                wa.append(t[:, 1, :])
+        def load_wl(g):
+            t = const.tile([P, 896], U32, name="wl%d" % g, align_bytes=64)
+            nc.sync.dma_start(out=t[:].bitcast(I32), in_=ww[:, g, 1024:1920])
+            wl[g] = t
 
-        def load_wbc(g):
-            t = const.tile([P, 1024], U32, name="wbc%d" % g, align_bytes=64)
-            nc.sync.dma_start(out=t[:].bitcast(I32), in_=ww[:, g, 512:1536])
-            wbc.append(t)
-
-        def load_wde(h):
-            t = const.tile([P, 5, 384], U32, name="wde%d" % h, align_bytes=64)
-            nc.sync.dma_start(out=t[:].bitcast(I32), in_=ww[:, 5 * h : 5 * h + 5, 1536:1920])
-            wde.append(t)
+        def load_wab(g):
+            t = const.tile([P, 1024], U32, name="wab%d" % g, align_bytes=64)
+            nc.sync.dma_start(out=t[:].bitcast(I32), in_=ww[:, g, 0:1024])
+            wab[g] = t
 
         load_x(0)
         load_x(1)
-        load_planes(pa, 0, 0, 512)
-        load_wa(0)
+        load_planes(ph, 0, 0, 1024)
+        load_wab(0)
+        load_wab(1)
         load_x(2)
-        load_planes(pa, 1, 0, 512)
-        load_wa(1)
+        load_wab(2)
+        load_wab(3)
         load_x(3)
-        load_wa(2)
+        load_planes(ph, 1, 0, 1024)
+        load_wab(4)
+        load_wab(5)
         load_x(4)
-        load_planes(pa, 2, 0, 512)
-        load_wa(3)
-        load_wa(4)
-        load_planes(pr, 0, 512, 1920)
+        load_wab(6)
+        load_wab(7)
+        load_planes(ph, 2, 0, 1024)
+        load_wab(8)
+        load_wab(9)
+        load_planes(pl, 0, 1024, 1920)
         for g in range(0, 4):
-            load_wbc(g)
-        load_planes(pr, 1, 512, 1920)
-        load_planes(pr, 2, 512, 1920)
+            load_wl(g)
+        load_planes(pl, 1, 1024, 1920)
+        load_planes(pl, 2, 1024, 1920)
         for g in range(4, PASSES):
-            load_wbc(g)
-        load_wde(0)
-        load_wde(1)
+            load_wl(g)
 
+        xs = {}
         xg = {}
         xq = {}
         xp = {}
+
+        def words(c, j):
+            return xr[(c, j)][:].rearrange("p m k -> p (m k)").bitcast(F32)
+
+        def sort(c):
+            for j in range(2):
+                t = xs_pool.tile([P, 4, 2, P], F32, tag="xs", name="xs%d_%d" % (c, j))
+                nc.scalar.copy(out=t[:], in_=words(c, j).rearrange("p (a q u) -> p a u q", a=4, q=P, u=2))
+                xs[(c, j)] = t
 
         def transposes(c):
             for gi in range(2):
                 g = 2 * c + gi
                 xg[g] = xg_pool.tile([P, 2048], BF16, tag="xg", name="xg%d" % g, align_bytes=64)
             for j in range(2):
-                xw = xr[(c, j)][:].rearrange("p m k -> p (m k)").bitcast(F32)
-                if c >= SORTED_FROM:
-                    xs = xs_pool.tile([P, 4, 2, P], F32, tag="xs", name="xs%d_%d" % (c, j))
-                    nc.vector.tensor_copy(out=xs[:], in_=xw.rearrange("p (a q u) -> p a u q", a=4, q=P, u=2))
                 for gi in range(2):
                     g = 2 * c + gi
                     bank = 2 * j + gi if c == 0 else 4 + 2 * j + gi
@@ -130,9 +128,9 @@ def tile_applypolicymap_kernel(tc, x, fc1_words, fc1_scales, out):
                         a = 2 * mi + gi
                         for u in range(2):
                             if c >= SORTED_FROM:
-                                src = xs[:, a, u, :]
+                                src = xs[(c, j)][:, a, u, :]
                             else:
-                                src = xw[:, 256 * a + u : 256 * (a + 1) : 2]
+                                src = words(c, j)[:, 256 * a + u : 256 * (a + 1) : 2]
                             nc.tensor.transpose(tb[:, mi, u, :], src, ident[:])
                     dst = xg[g][:].bitcast(F32).rearrange("p (m r u) -> p m r u", m=4, r=P, u=2)
                     nc.scalar.copy(out=dst[:, 2 * j : 2 * j + 2], in_=tb[:].rearrange("p m u r -> p m r u"))
@@ -144,7 +142,7 @@ def tile_applypolicymap_kernel(tc, x, fc1_words, fc1_scales, out):
                 xp[g] = const.tile([P, ROWS], U8, name="xp%d" % g, align_bytes=64)
                 nc.vector.quantize_mx(out=xq[g][:].bitcast(FP8X4), scales=xp[g][:], in_=xg[g][:])
 
-        def mx(acc, g, m, rhs, planes, col0, width):
+        def mx(acc, g, m, rhs, planes, col0, width, first, last):
             k = 4 * (g % 4)
             nc.tensor.matmul_mx(
                 out=acc,
@@ -152,9 +150,12 @@ def tile_applypolicymap_kernel(tc, x, fc1_words, fc1_scales, out):
                 lhsT_scale=xp[g][:, P * m : P * (m + 1)],
                 rhs=rhs.bitcast(FP8X4),
                 rhs_scale=planes[g // 4][k:P, col0 : col0 + width],
-                start=(g == 0),
-                stop=(g == PASSES - 1),
+                start=first,
+                stop=last,
             )
+
+        def store(src, m, n0, width):
+            nc.sync.dma_start(out=out[P * m : P * (m + 1), n0 : n0 + width], in_=src)
 
         def evacuate(acc, m, n0, width, on_scalar):
             ob = const.tile([P, width], F32, name="ob%d_%d" % (m, n0))
@@ -162,39 +163,58 @@ def tile_applypolicymap_kernel(tc, x, fc1_words, fc1_scales, out):
                 nc.scalar.copy(out=ob[:], in_=acc)
             else:
                 nc.vector.tensor_copy(out=ob[:], in_=acc)
-            nc.sync.dma_start(out=out[P * m : P * (m + 1), n0 : n0 + width], in_=ob[:])
+            store(ob[:], m, n0, width)
 
         transposes(0)
         transposes(1)
+        quantise(0)
         acc_a = [psum.tile([P, 512], F32, tag="bank%d" % m, name="accA%d" % m) for m in range(M_TILES)]
+        part_b = [None] * M_TILES
         for c in range(N_CHUNKS):
-            quantise(c)
-            for gi in range(2):
-                for m in range(M_TILES):
-                    mx(acc_a[m][:], 2 * c + gi, m, wa[2 * c + gi], pa, 0, 512)
+            g0 = 2 * c
+            g1 = g0 + 1
+            for m in range(M_TILES):
+                mx(acc_a[m][:], g0, m, wab[g0][:, 0:512], ph, 0, 512, g0 == 0, False)
+            acc_b = [
+                psum.tile([P, 512], F32, tag="bank%d" % (4 + m), name="accB%d_%d" % (c, m)) for m in range(M_TILES)
+            ]
+            for m in range(M_TILES):
+                mx(acc_b[m][:], g0, m, wab[g0][:, 512:1024], ph, 512, 512, True, False)
+            for m in range(M_TILES):
+                mx(acc_b[m][:], g1, m, wab[g1][:, 512:1024], ph, 512, 512, False, True)
+            for m in range(M_TILES):
+                mx(acc_a[m][:], g1, m, wab[g1][:, 0:512], ph, 0, 512, False, g1 == PASSES - 1)
+            if c + 1 < N_CHUNKS:
+                quantise(c + 1)
+            if c + 2 < N_CHUNKS:
+                sort(c + 2)
+            for m in range(M_TILES):
+                t = pb_pool.tile([P, 512], F32, tag="pb%d" % m, name="pb%d_%d" % (m, c))
+                if c == 0:
+                    nc.vector.tensor_copy(out=t[:], in_=acc_b[m][:])
+                else:
+                    nc.vector.tensor_tensor(out=t[:], in0=acc_b[m][:], in1=part_b[m][:], op=ADD)
+                part_b[m] = t
             if c + 2 < N_CHUNKS:
                 transposes(c + 2)
         for m in range(M_TILES):
+            store(part_b[m][:], m, 512, 512)
+        for m in range(M_TILES):
             evacuate(acc_a[m][:], m, 0, 512, m % 2 == 0)
 
-        acc_b = [psum.tile([P, 512], F32, tag="bank%d" % (4 + m), name="accB%d" % m) for m in range(M_TILES)]
-        acc_c = [psum.tile([P, 512], F32, tag="bank%d" % m, name="accC%d" % m) for m in range(M_TILES)]
+        acc_c = [psum.tile([P, 512], F32, tag="bank%d" % (4 + m), name="accC%d" % m) for m in range(M_TILES)]
         for g in range(PASSES):
             for m in range(M_TILES):
-                mx(acc_b[m][:], g, m, wbc[g][:, 0:512], pr, 0, 512)
-            for m in range(M_TILES):
-                mx(acc_c[m][:], g, m, wbc[g][:, 512:1024], pr, 512, 512)
-        for m in range(M_TILES):
-            evacuate(acc_b[m][:], m, 512, 512, m % 2 == 0)
+                mx(acc_c[m][:], g, m, wl[g][:, 0:512], pl, 0, 512, g == 0, g == PASSES - 1)
         for m in range(M_TILES):
             evacuate(acc_c[m][:], m, 1024, 512, m % 2 == 0)
 
         for m in range(M_TILES):
-            acc_d = psum.tile([P, 256], F32, tag="bank%d" % (4 + m), name="accD%d" % m)
+            acc_d = psum.tile([P, 256], F32, tag="bank%d" % m, name="accD%d" % m)
             for g in range(PASSES):
-                mx(acc_d[:], g, m, wde[g // 5][:, g % 5, 0:256], pr, 1024, 256)
-            acc_e = psum.tile([P, 128], F32, tag="bank%d" % m, name="accE%d" % m)
+                mx(acc_d[:], g, m, wl[g][:, 512:768], pl, 512, 256, g == 0, g == PASSES - 1)
+            acc_e = psum.tile([P, 128], F32, tag="bank%d" % (4 + m), name="accE%d" % m)
             for g in range(PASSES):
-                mx(acc_e[:], g, m, wde[g // 5][:, g % 5, 256:384], pr, 1280, 128)
+                mx(acc_e[:], g, m, wl[g][:, 768:896], pl, 768, 128, g == 0, g == PASSES - 1)
             evacuate(acc_d[:], m, 1536, 256, True)
             evacuate(acc_e[:], m, 1792, 128, False)

@@ -9,7 +9,6 @@ F32 = mybir.dt.float32
 I32 = mybir.dt.int32
 U32 = mybir.dt.uint32
 U8 = mybir.dt.uint8
-ADD = mybir.AluOpType.add
 
 P = 128
 ROWS = 512
@@ -20,6 +19,7 @@ M_TILES = 4
 FLOPS = 2 * ROWS * K * N_OUT
 
 N_CHUNKS = 5
+PAD = 48
 SORTED_FROM = 2
 
 
@@ -32,7 +32,6 @@ def tile_applypolicymap_kernel(tc, x, fc1_words, fc1_scales, out):
         const = ctx.enter_context(tc.tile_pool(name="const", bufs=1))
         xs_pool = ctx.enter_context(tc.tile_pool(name="xs", bufs=4))
         xg_pool = ctx.enter_context(tc.tile_pool(name="xg", bufs=4))
-        pb_pool = ctx.enter_context(tc.tile_pool(name="pb", bufs=2))
         psum = ctx.enter_context(tc.psum_pool(name="psum", bufs=1))
         ctx.enter_context(tc.manual_schedule())
 
@@ -40,16 +39,17 @@ def tile_applypolicymap_kernel(tc, x, fc1_words, fc1_scales, out):
         warm_out = const.tile([P, 1], F32, name="warm_out")
         nc.vector.memset(warm_in[:], 0.0)
         nc.scalar.copy(out=warm_out[:], in_=warm_in[:])
-        ph = [const.tile([P, 1024], U8, name="ph%d" % s, align_bytes=64) for s in range(3)]
-        pl = [const.tile([P, 896], U8, name="pl%d" % s, align_bytes=64) for s in range(3)]
-        for t in ph + pl:
+        pa = [const.tile([P, 512], U8, name="pa%d" % s, align_bytes=256) for s in range(3)]
+        pr = [const.tile([P, 1408], U8, name="pr%d" % s, align_bytes=256) for s in range(3)]
+        for t in pa + pr:
             nc.vector.memset(t[:].bitcast(I32), 0)
         ident = const.tile([P, P], F32, name="ident")
         make_identity(nc, ident[:])
 
         xr = {}
-        wl = {}
-        wab = {}
+        wa = []
+        wbc = []
+        wde = []
 
         def load_x(c):
             for j in range(2):
@@ -65,61 +65,64 @@ def tile_applypolicymap_kernel(tc, x, fc1_words, fc1_scales, out):
                     in_=fc1_scales[4 * s : 4 * s + n_planes, 4 * q : 4 * q + 4, c0:c1].bitcast(I32),
                 )
 
-        def load_wl(g):
-            t = const.tile([P, 896], U32, name="wl%d" % g, align_bytes=64)
-            nc.sync.dma_start(out=t[:].bitcast(I32), in_=ww[:, g, 1024:1920])
-            wl[g] = t
+        def load_wa(c):
+            if c == 0:
+                for g in range(2):
+                    t = const.tile([P, 512], U32, name="wa0_%d" % g, align_bytes=256)
+                    nc.sync.dma_start(out=t[:].bitcast(I32), in_=ww[:, g, 0:512])
+                    wa.append(t[:])
+            else:
+                t = const.tile([P, 2, 512], U32, name="wa%d" % c, align_bytes=256)
+                nc.sync.dma_start(out=t[:].bitcast(I32), in_=ww[:, 2 * c : 2 * c + 2, 0:512])
+                wa.append(t[:, 0, :])
+                wa.append(t[:, 1, :])
 
-        def load_wab(g):
-            t = const.tile([P, 1024], U32, name="wab%d" % g, align_bytes=64)
-            nc.sync.dma_start(out=t[:].bitcast(I32), in_=ww[:, g, 0:1024])
-            wab[g] = t
+        def load_wbc(g):
+            t = const.tile([P, 1024], U32, name="wbc%d" % g, align_bytes=256)
+            nc.sync.dma_start(out=t[:].bitcast(I32), in_=ww[:, g, 512:1536])
+            wbc.append(t)
+
+        def load_wde(h):
+            t = const.tile([P, 5, 384], U32, name="wde%d" % h, align_bytes=256)
+            nc.sync.dma_start(out=t[:].bitcast(I32), in_=ww[:, 5 * h : 5 * h + 5, 1536:1920])
+            wde.append(t)
 
         load_x(0)
         load_x(1)
-        load_planes(ph, 0, 0, 1024)
-        load_wab(0)
-        load_wab(1)
+        load_planes(pa, 0, 0, 512)
+        load_wa(0)
         load_x(2)
-        load_wab(2)
-        load_wab(3)
+        load_planes(pa, 1, 0, 512)
+        load_wa(1)
         load_x(3)
-        load_planes(ph, 1, 0, 1024)
-        load_wab(4)
-        load_wab(5)
+        load_wa(2)
         load_x(4)
-        load_wab(6)
-        load_wab(7)
-        load_planes(ph, 2, 0, 1024)
-        load_wab(8)
-        load_wab(9)
-        load_planes(pl, 0, 1024, 1920)
+        load_planes(pa, 2, 0, 512)
+        load_wa(3)
+        load_wa(4)
+        load_planes(pr, 0, 512, 1920)
         for g in range(0, 4):
-            load_wl(g)
-        load_planes(pl, 1, 1024, 1920)
-        load_planes(pl, 2, 1024, 1920)
+            load_wbc(g)
+        load_planes(pr, 1, 512, 1920)
+        load_planes(pr, 2, 512, 1920)
         for g in range(4, PASSES):
-            load_wl(g)
+            load_wbc(g)
+        load_wde(0)
+        load_wde(1)
 
-        xs = {}
         xg = {}
         xq = {}
         xp = {}
-
-        def words(c, j):
-            return xr[(c, j)][:].rearrange("p m k -> p (m k)").bitcast(F32)
-
-        def sort(c):
-            for j in range(2):
-                t = xs_pool.tile([P, 4, 2, P], F32, tag="xs", name="xs%d_%d" % (c, j))
-                nc.scalar.copy(out=t[:], in_=words(c, j).rearrange("p (a q u) -> p a u q", a=4, q=P, u=2))
-                xs[(c, j)] = t
 
         def transposes(c):
             for gi in range(2):
                 g = 2 * c + gi
                 xg[g] = xg_pool.tile([P, 2048], BF16, tag="xg", name="xg%d" % g, align_bytes=64)
             for j in range(2):
+                xw = xr[(c, j)][:].rearrange("p m k -> p (m k)").bitcast(F32)
+                if c >= SORTED_FROM:
+                    xs = xs_pool.tile([P, 4, 2, P], F32, tag="xs", name="xs%d_%d" % (c, j))
+                    nc.vector.tensor_copy(out=xs[:], in_=xw.rearrange("p (a q u) -> p a u q", a=4, q=P, u=2))
                 for gi in range(2):
                     g = 2 * c + gi
                     bank = 2 * j + gi if c == 0 else 4 + 2 * j + gi
@@ -128,9 +131,9 @@ def tile_applypolicymap_kernel(tc, x, fc1_words, fc1_scales, out):
                         a = 2 * mi + gi
                         for u in range(2):
                             if c >= SORTED_FROM:
-                                src = xs[(c, j)][:, a, u, :]
+                                src = xs[:, a, u, :]
                             else:
-                                src = words(c, j)[:, 256 * a + u : 256 * (a + 1) : 2]
+                                src = xw[:, 256 * a + u : 256 * (a + 1) : 2]
                             nc.tensor.transpose(tb[:, mi, u, :], src, ident[:])
                     dst = xg[g][:].bitcast(F32).rearrange("p (m r u) -> p m r u", m=4, r=P, u=2)
                     nc.scalar.copy(out=dst[:, 2 * j : 2 * j + 2], in_=tb[:].rearrange("p m u r -> p m r u"))
@@ -138,24 +141,26 @@ def tile_applypolicymap_kernel(tc, x, fc1_words, fc1_scales, out):
         def quantise(c):
             for gi in range(2):
                 g = 2 * c + gi
-                xq[g] = const.tile([P, ROWS], U32, name="xq%d" % g, align_bytes=64)
-                xp[g] = const.tile([P, ROWS], U8, name="xp%d" % g, align_bytes=64)
-                nc.vector.quantize_mx(out=xq[g][:].bitcast(FP8X4), scales=xp[g][:], in_=xg[g][:])
+                xq[g] = const.tile([P, PAD + ROWS], U32, name="xq%d" % g, align_bytes=256)
+                xp[g] = const.tile([P, M_TILES, 256], U8, name="xp%d" % g, align_bytes=256)
+                for m in range(M_TILES):
+                    nc.vector.quantize_mx(
+                        out=xq[g][:, PAD + P * m : PAD + P * (m + 1)].bitcast(FP8X4),
+                        scales=xp[g][:, m, 0:P],
+                        in_=xg[g][:, 4 * P * m : 4 * P * (m + 1)],
+                    )
 
-        def mx(acc, g, m, rhs, planes, col0, width, first, last):
+        def mx(acc, g, m, rhs, planes, col0, width):
             k = 4 * (g % 4)
             nc.tensor.matmul_mx(
                 out=acc,
-                lhsT=xq[g][:, P * m : P * (m + 1)].bitcast(FP8X4),
-                lhsT_scale=xp[g][:, P * m : P * (m + 1)],
+                lhsT=xq[g][:, PAD + P * m : PAD + P * (m + 1)].bitcast(FP8X4),
+                lhsT_scale=xp[g][:, m, 0:P],
                 rhs=rhs.bitcast(FP8X4),
                 rhs_scale=planes[g // 4][k:P, col0 : col0 + width],
-                start=first,
-                stop=last,
+                start=(g == 0),
+                stop=(g == PASSES - 1),
             )
-
-        def store(src, m, n0, width):
-            nc.sync.dma_start(out=out[P * m : P * (m + 1), n0 : n0 + width], in_=src)
 
         def evacuate(acc, m, n0, width, on_scalar):
             ob = const.tile([P, width], F32, name="ob%d_%d" % (m, n0))
@@ -163,58 +168,39 @@ def tile_applypolicymap_kernel(tc, x, fc1_words, fc1_scales, out):
                 nc.scalar.copy(out=ob[:], in_=acc)
             else:
                 nc.vector.tensor_copy(out=ob[:], in_=acc)
-            store(ob[:], m, n0, width)
+            nc.sync.dma_start(out=out[P * m : P * (m + 1), n0 : n0 + width], in_=ob[:])
 
         transposes(0)
         transposes(1)
-        quantise(0)
         acc_a = [psum.tile([P, 512], F32, tag="bank%d" % m, name="accA%d" % m) for m in range(M_TILES)]
-        part_b = [None] * M_TILES
         for c in range(N_CHUNKS):
-            g0 = 2 * c
-            g1 = g0 + 1
-            for m in range(M_TILES):
-                mx(acc_a[m][:], g0, m, wab[g0][:, 0:512], ph, 0, 512, g0 == 0, False)
-            acc_b = [
-                psum.tile([P, 512], F32, tag="bank%d" % (4 + m), name="accB%d_%d" % (c, m)) for m in range(M_TILES)
-            ]
-            for m in range(M_TILES):
-                mx(acc_b[m][:], g0, m, wab[g0][:, 512:1024], ph, 512, 512, True, False)
-            for m in range(M_TILES):
-                mx(acc_b[m][:], g1, m, wab[g1][:, 512:1024], ph, 512, 512, False, True)
-            for m in range(M_TILES):
-                mx(acc_a[m][:], g1, m, wab[g1][:, 0:512], ph, 0, 512, False, g1 == PASSES - 1)
-            if c + 1 < N_CHUNKS:
-                quantise(c + 1)
-            if c + 2 < N_CHUNKS:
-                sort(c + 2)
-            for m in range(M_TILES):
-                t = pb_pool.tile([P, 512], F32, tag="pb%d" % m, name="pb%d_%d" % (m, c))
-                if c == 0:
-                    nc.vector.tensor_copy(out=t[:], in_=acc_b[m][:])
-                else:
-                    nc.vector.tensor_tensor(out=t[:], in0=acc_b[m][:], in1=part_b[m][:], op=ADD)
-                part_b[m] = t
+            quantise(c)
+            for gi in range(2):
+                for m in range(M_TILES):
+                    mx(acc_a[m][:], 2 * c + gi, m, wa[2 * c + gi], pa, 0, 512)
             if c + 2 < N_CHUNKS:
                 transposes(c + 2)
         for m in range(M_TILES):
-            store(part_b[m][:], m, 512, 512)
-        for m in range(M_TILES):
             evacuate(acc_a[m][:], m, 0, 512, m % 2 == 0)
 
-        acc_c = [psum.tile([P, 512], F32, tag="bank%d" % (4 + m), name="accC%d" % m) for m in range(M_TILES)]
+        acc_b = [psum.tile([P, 512], F32, tag="bank%d" % (4 + m), name="accB%d" % m) for m in range(M_TILES)]
+        acc_c = [psum.tile([P, 512], F32, tag="bank%d" % m, name="accC%d" % m) for m in range(M_TILES)]
         for g in range(PASSES):
             for m in range(M_TILES):
-                mx(acc_c[m][:], g, m, wl[g][:, 0:512], pl, 0, 512, g == 0, g == PASSES - 1)
+                mx(acc_b[m][:], g, m, wbc[g][:, 0:512], pr, 0, 512)
+            for m in range(M_TILES):
+                mx(acc_c[m][:], g, m, wbc[g][:, 512:1024], pr, 512, 512)
+        for m in range(M_TILES):
+            evacuate(acc_b[m][:], m, 512, 512, m % 2 == 0)
         for m in range(M_TILES):
             evacuate(acc_c[m][:], m, 1024, 512, m % 2 == 0)
 
         for m in range(M_TILES):
-            acc_d = psum.tile([P, 256], F32, tag="bank%d" % m, name="accD%d" % m)
+            acc_d = psum.tile([P, 256], F32, tag="bank%d" % (4 + m), name="accD%d" % m)
             for g in range(PASSES):
-                mx(acc_d[:], g, m, wl[g][:, 512:768], pl, 512, 256, g == 0, g == PASSES - 1)
-            acc_e = psum.tile([P, 128], F32, tag="bank%d" % (4 + m), name="accE%d" % m)
+                mx(acc_d[:], g, m, wde[g // 5][:, g % 5, 0:256], pr, 1024, 256)
+            acc_e = psum.tile([P, 128], F32, tag="bank%d" % m, name="accE%d" % m)
             for g in range(PASSES):
-                mx(acc_e[:], g, m, wl[g][:, 768:896], pl, 768, 128, g == 0, g == PASSES - 1)
+                mx(acc_e[:], g, m, wde[g // 5][:, g % 5, 256:384], pr, 1280, 128)
             evacuate(acc_d[:], m, 1536, 256, True)
             evacuate(acc_e[:], m, 1792, 128, False)

from contextlib import ExitStack

import concourse.mybir as mybir
from concourse.masks import make_identity

FP8X4 = mybir.dt.float8_e4m3fn_x4
BF16 = mybir.dt.bfloat16
F32 = mybir.dt.float32
I32 = mybir.dt.int32
U32 = mybir.dt.uint32
U8 = mybir.dt.uint8

P = 128
ROWS = 512
K = 5120
N_OUT = 1920
PASSES = 10
M_TILES = 4
FLOPS = 2 * ROWS * K * N_OUT

N_CHUNKS = 5
PAD = 48
SORTED_FROM = 2


def tile_applypolicymap_kernel(tc, x, fc1_words, fc1_scales, out):
    nc = tc.nc
    xf = x.rearrange("(m p) c h w -> p m (c h w)", p=P)
    ww = fc1_words.rearrange("g p n t -> g p (n t)").bitcast(I32).rearrange("g p n -> p g n")

    with ExitStack() as ctx:
        const = ctx.enter_context(tc.tile_pool(name="const", bufs=1))
        xs_pool = ctx.enter_context(tc.tile_pool(name="xs", bufs=4))
        xg_pool = ctx.enter_context(tc.tile_pool(name="xg", bufs=4))
        psum = ctx.enter_context(tc.psum_pool(name="psum", bufs=1))
        ctx.enter_context(tc.manual_schedule())

        warm_in = const.tile([P, 1], F32, name="warm_in")
        warm_out = const.tile([P, 1], F32, name="warm_out")
        nc.vector.memset(warm_in[:], 0.0)
        nc.scalar.copy(out=warm_out[:], in_=warm_in[:])
        pa = [const.tile([P, 512], U8, name="pa%d" % s, align_bytes=256) for s in range(3)]
        pr = [const.tile([P, 1408], U8, name="pr%d" % s, align_bytes=256) for s in range(3)]
        for t in pa + pr:
            nc.vector.memset(t[:].bitcast(I32), 0)
        ident = const.tile([P, P], F32, name="ident")
        make_identity(nc, ident[:])

        xr = {}
        wa = []
        wbc = []
        wde = []

        def load_x(c):
            for j in range(2):
                t = const.tile([P, 2, 1024], BF16, name="xr%d_%d" % (c, j))
                nc.sync.dma_start(out=t[:], in_=xf[:, 2 * j : 2 * j + 2, 1024 * c : 1024 * (c + 1)])
                xr[(c, j)] = t

        def load_planes(tiles, s, c0, c1):
            n_planes = min(4, PASSES - 4 * s)
            for q in range(4):
                nc.sync.dma_start(
                    out=tiles[s][32 * q : 32 * q + 4 * n_planes, :].bitcast(I32),
                    in_=fc1_scales[4 * s : 4 * s + n_planes, 4 * q : 4 * q + 4, c0:c1].bitcast(I32),
                )

        def load_wa(c):
            if c == 0:
                for g in range(2):
                    t = const.tile([P, 512], U32, name="wa0_%d" % g, align_bytes=256)
                    nc.sync.dma_start(out=t[:].bitcast(I32), in_=ww[:, g, 0:512])
                    wa.append(t[:])
            else:
                t = const.tile([P, 2, 512], U32, name="wa%d" % c, align_bytes=256)
                nc.sync.dma_start(out=t[:].bitcast(I32), in_=ww[:, 2 * c : 2 * c + 2, 0:512])
                wa.append(t[:, 0, :])
                wa.append(t[:, 1, :])

        def load_wbc(g):
            t = const.tile([P, 1024], U32, name="wbc%d" % g, align_bytes=256)
            nc.sync.dma_start(out=t[:].bitcast(I32), in_=ww[:, g, 512:1536])
            wbc.append(t)

        def load_wde(h):
            t = const.tile([P, 5, 384], U32, name="wde%d" % h, align_bytes=256)
            nc.sync.dma_start(out=t[:].bitcast(I32), in_=ww[:, 5 * h : 5 * h + 5, 1536:1920])
            wde.append(t)

        load_x(0)
        load_x(1)
        load_planes(pa, 0, 0, 512)
        load_wa(0)
        load_x(2)
        load_planes(pa, 1, 0, 512)
        load_wa(1)
        load_x(3)
        load_wa(2)
        load_x(4)
        load_planes(pa, 2, 0, 512)
        load_wa(3)
        load_wa(4)
        load_planes(pr, 0, 512, 1920)
        for g in range(0, 4):
            load_wbc(g)
        load_planes(pr, 1, 512, 1920)
        load_planes(pr, 2, 512, 1920)
        for g in range(4, PASSES):
            load_wbc(g)
        load_wde(0)
        load_wde(1)

        xg = {}
        xq = {}
        xp = {}

        def transposes(c):
            for gi in range(2):
                g = 2 * c + gi
                xg[g] = xg_pool.tile([P, 2048], BF16, tag="xg", name="xg%d" % g, align_bytes=64)
            for j in range(2):
                xw = xr[(c, j)][:].rearrange("p m k -> p (m k)").bitcast(F32)
                if c >= SORTED_FROM:
                    xs = xs_pool.tile([P, 4, 2, P], F32, tag="xs", name="xs%d_%d" % (c, j))
                    nc.vector.tensor_copy(out=xs[:], in_=xw.rearrange("p (a q u) -> p a u q", a=4, q=P, u=2))
                for gi in range(2):
                    g = 2 * c + gi
                    bank = 2 * j + gi if c == 0 else 4 + 2 * j + gi
                    tb = psum.tile([P, 2, 2, P], F32, tag="bank%d" % bank, name="tb%d_%d" % (g, j))
                    for mi in range(2):
                        a = 2 * mi + gi
                        for u in range(2):
                            if c >= SORTED_FROM:
                                src = xs[:, a, u, :]
                            else:
                                src = xw[:, 256 * a + u : 256 * (a + 1) : 2]
                            nc.tensor.transpose(tb[:, mi, u, :], src, ident[:])
                    dst = xg[g][:].bitcast(F32).rearrange("p (m r u) -> p m r u", m=4, r=P, u=2)
                    nc.scalar.copy(out=dst[:, 2 * j : 2 * j + 2], in_=tb[:].rearrange("p m u r -> p m r u"))

        def quantise(c):
            for gi in range(2):
                g = 2 * c + gi
                xq[g] = const.tile([P, PAD + ROWS], U32, name="xq%d" % g, align_bytes=256)
                xp[g] = const.tile([P, M_TILES, 256], U8, name="xp%d" % g, align_bytes=256)
                for m in range(M_TILES):
                    nc.vector.quantize_mx(
                        out=xq[g][:, PAD + P * m : PAD + P * (m + 1)].bitcast(FP8X4),
                        scales=xp[g][:, m, 0:P],
                        in_=xg[g][:, 4 * P * m : 4 * P * (m + 1)],
                    )

        def mx(acc, g, m, rhs, planes, col0, width):
            k = 4 * (g % 4)
            nc.tensor.matmul_mx(
                out=acc,
                lhsT=xq[g][:, PAD + P * m : PAD + P * (m + 1)].bitcast(FP8X4),
                lhsT_scale=xp[g][:, m, 0:P],
                rhs=rhs.bitcast(FP8X4),
                rhs_scale=planes[g // 4][k:P, col0 : col0 + width],
                start=(g == 0),
                stop=(g == PASSES - 1),
            )

        def evacuate(acc, m, n0, width, on_scalar):
            ob = const.tile([P, width], F32, name="ob%d_%d" % (m, n0))
            if on_scalar:
                nc.scalar.copy(out=ob[:], in_=acc)
            else:
                nc.vector.tensor_copy(out=ob[:], in_=acc)
            nc.sync.dma_start(out=out[P * m : P * (m + 1), n0 : n0 + width], in_=ob[:])

        transposes(0)
        transposes(1)
        acc_a = [psum.tile([P, 512], F32, tag="bank%d" % m, name="accA%d" % m) for m in range(M_TILES)]
        for c in range(N_CHUNKS):
            quantise(c)
            for gi in range(2):
                for m in range(M_TILES):
                    mx(acc_a[m][:], 2 * c + gi, m, wa[2 * c + gi], pa, 0, 512)
            if c + 2 < N_CHUNKS:
                transposes(c + 2)
        for m in range(M_TILES):
            evacuate(acc_a[m][:], m, 0, 512, m % 2 == 0)

        acc_b = [psum.tile([P, 512], F32, tag="bank%d" % (4 + m), name="accB%d" % m) for m in range(M_TILES)]
        acc_c = [psum.tile([P, 512], F32, tag="bank%d" % m, name="accC%d" % m) for m in range(M_TILES)]
        for g in range(PASSES):
            for m in range(M_TILES):
                mx(acc_b[m][:], g, m, wbc[g][:, 0:512], pr, 0, 512)
            for m in range(M_TILES):
                mx(acc_c[m][:], g, m, wbc[g][:, 512:1024], pr, 512, 512)
        for m in range(M_TILES):
            evacuate(acc_b[m][:], m, 512, 512, m % 2 == 0)
        for m in range(M_TILES):
            evacuate(acc_c[m][:], m, 1024, 512, m % 2 == 0)

        for m in range(M_TILES):
            acc_d = psum.tile([P, 256], F32, tag="bank%d" % (4 + m), name="accD%d" % m)
            for g in range(PASSES):
                mx(acc_d[:], g, m, wde[g // 5][:, g % 5, 0:256], pr, 1024, 256)
            acc_e = psum.tile([P, 128], F32, tag="bank%d" % m, name="accE%d" % m)
            for g in range(PASSES):
                mx(acc_e[:], g, m, wde[g // 5][:, g % 5, 256:384], pr, 1280, 128)
            evacuate(acc_d[:], m, 1536, 256, True)
            evacuate(acc_e[:], m, 1792, 128, False)
